import numpy as np
import ml_dtypes


def mxq(x, axis, fmt="e4m3"):
    dtype, down = {"e4m3": (ml_dtypes.float8_e4m3fn, 7), "e5m2": (ml_dtypes.float8_e5m2, 14)}[fmt]
    v = np.moveaxis(np.asarray(x, np.float32).astype(ml_dtypes.bfloat16).astype(np.float64), axis, -1)
    blocks = v.reshape(v.shape[:-1] + (-1, 32))
    amax = np.abs(blocks).max(-1, keepdims=True)
    byte = np.maximum(np.where(amax > 0, np.frexp(amax)[1] - 1 + 127, 0) - down, 1)
    scale = np.exp2(byte - 127.0)
    codes = (blocks / scale).astype(np.float32).astype(dtype).astype(np.float64)
    return np.moveaxis((codes * scale).reshape(v.shape), -1, axis)


WIDE = False


def mx_kscale(k):
    if not WIDE:
        return np.ones(k)
    levels = np.array([10, -10, 5, -5, 0])
    if k % 512:
        return np.exp2(np.random.permutation(np.resize(levels, k // 32))).repeat(32)
    a = np.empty((k // 512, 16))
    for p in range(k // 512):
        a[p, :8] = np.random.permutation(np.resize(levels, 8))
        for g in range(8):
            far = levels[np.abs(levels - a[p, g]) >= 10]
            a[p, g + 8] = far[np.random.randint(len(far))]
    return np.exp2(a.ravel()).repeat(32)


BF16 = ml_dtypes.bfloat16


def bf(x):
    return np.asarray(x, np.float32).astype(BF16)


def f64(x):
    return np.asarray(x).astype(np.float64)


E2M1 = np.array([0.0, 0.5, 1.0, 1.5, 2.0, 3.0, 4.0, 6.0, -0.0, -0.5, -1.0, -1.5, -2.0, -3.0, -4.0, -6.0])


def pack_weight(w, fmt):
    k, n = w.shape
    w = f64(bf(w)).reshape(k // 32, 32, n)
    amax = np.abs(w).max(1)
    if fmt == "e4m3":
        byte = np.frexp(amax)[1] - 1 + 127 - 7
    else:
        mant, ex = np.frexp(amax / 6.0)
        byte = np.where(mant > 0.5, ex, ex - 1) + 127
    byte = np.clip(np.where(amax > 0, byte, 1), 1, 254)
    scaled = (w * np.exp2(127.0 - byte)[:, None, :]).reshape(k, n).astype(np.float32)
    by_word = np.ascontiguousarray(scaled.reshape(k // 512, 128, 4, n).transpose(0, 1, 3, 2))
    if fmt == "e4m3":
        words = by_word.astype(ml_dtypes.float8_e4m3fn).view(np.uint8)
    else:
        c = by_word.astype(ml_dtypes.float4_e2m1fn).view(np.uint8) & 0xF
        words = c[..., 0::2] | (c[..., 1::2] << 4)
    return np.ascontiguousarray(words), np.ascontiguousarray(byte.astype(np.uint8).reshape(k // 512, 16, n))


def unpack_weight(words, scales, fmt):
    g, p, n, _ = words.shape
    if fmt == "e4m3":
        vals = np.ascontiguousarray(words).view(ml_dtypes.float8_e4m3fn).astype(np.float64)
    else:
        nib = np.empty((g, p, n, 4), np.uint8)
        nib[..., 0::2] = words & 0xF
        nib[..., 1::2] = words >> 4
        vals = E2M1[nib]
    vals = vals * np.repeat(np.exp2(scales.astype(np.float64) - 127.0), 8, axis=1)[..., None]
    return vals.transpose(0, 1, 3, 2).reshape(g * 512, n)


B, D, E, NM = 512, 1024, 1024, 4


def draw0():
    s, t = mx_kscale(D), mx_kscale(D)
    gain = np.ones((E, NM))
    gain[:, 1] = 0.3
    off = np.zeros((E, NM))
    off[:, 1] = 1.3 * np.sign(np.random.standard_normal(E))
    prev_act = bf(np.maximum(np.random.standard_normal((B, D)) * 1.2, 0.0) * s)
    W1_words, W1_scales = pack_weight(np.random.standard_normal((D, D)) / np.sqrt(D) / s[:, None] * t, "e4m3")
    b1 = bf(np.random.standard_normal(D) * 0.2 * t)
    W2_words, W2_scales = pack_weight(np.random.standard_normal((D, NM * E)) / np.sqrt(D) * gain.reshape(-1) / t[:, None], "e4m3")
    return {
        "prev_act": prev_act,
        "W1_words": W1_words,
        "W1_scales": W1_scales,
        "b1": b1,
        "W2_words": W2_words,
        "W2_scales": W2_scales,
        "b2": bf(np.random.standard_normal(NM * E) * 0.1 + off.reshape(-1)),
        "dopamine": bf(np.random.standard_normal((B, E))),
        "serotonin": bf(np.random.standard_normal((B, E))),
        "glutamate": bf(np.random.standard_normal((B, E))),
        "gaba": bf(np.random.standard_normal((B, E))),
    }


def core(prev_act, W1_words, W1_scales, b1, W2_words, W2_scales, b2, dopamine, serotonin, glutamate, gaba):
    hid = np.maximum((mxq(f64(prev_act), 1, "e4m3") @ unpack_weight(W1_words, W1_scales, "e4m3")) + f64(b1), 0.0)
    h = np.tanh((mxq(hid, 1, "e4m3") @ unpack_weight(W2_words, W2_scales, "e4m3")) + f64(b2))
    preds = h.reshape(B, E, NM)
    p_dop, p_ser, p_glu, p_gab = preds[..., 0], preds[..., 1], preds[..., 2], preds[..., 3]
    inv = 1.0 / np.maximum(np.abs(p_ser), 1e-6)
    dop = f64(dopamine) + p_dop * inv
    ser = f64(serotonin) + p_ser
    glu = f64(glutamate) + p_glu * inv
    gab = f64(gaba) + p_gab * inv
    return np.concatenate([dop, ser, glu, gab], axis=0)


def e4m3fn_bytes(y):
    return np.clip(np.asarray(y, np.float64), -448.0, 448.0).astype(np.float32).astype(ml_dtypes.float8_e4m3fn).view(np.uint8)


def e4m3fn_values(b):
    return np.asarray(b, np.uint8).view(ml_dtypes.float8_e4m3fn).astype(np.float64)


def setup_inputs():
    d = draw0()
    x0 = np.asarray(d['prev_act']).astype(np.float64)
    s = (np.max(np.abs(x0), axis=(0,), keepdims=True) / 448.0).astype(np.float32)
    out = {}
    for k, v in d.items():
        if k == 'prev_act':
            out['prev_act_bytes'] = e4m3fn_bytes(x0 / s.astype(np.float64))
            out['prev_act_scale'] = s
        else:
            out[k] = v
    return out


def reference(prev_act_bytes, prev_act_scale, W1_words, W1_scales, b1, W2_words, W2_scales, b2, dopamine, serotonin, glutamate, gaba):
    return core(e4m3fn_values(prev_act_bytes) * prev_act_scale.astype(np.float64), W1_words, W1_scales, b1, W2_words, W2_scales, b2, dopamine, serotonin, glutamate, gaba)

@@ -1,0 +1,377 @@
+from contextlib import ExitStack
+
+import concourse.mybir as mybir
+from concourse.masks import make_identity
+
+F32 = mybir.dt.float32
+BF16 = mybir.dt.bfloat16
+I32 = mybir.dt.int32
+U32 = mybir.dt.uint32
+U8 = mybir.dt.uint8
+FP8 = mybir.dt.float8_e4m3fn
+FP8X4 = mybir.dt.float8_e4m3fn_x4
+ACT = mybir.ActivationFunctionType
+ALU = mybir.AluOpType
+
+P = 128
+B, D, E, NM = 512, 1024, 1024, 4
+FLOPS = 2 * B * D * D + 2 * B * D * NM * E
+DOP, SER, GLU, GAB = 0, 1, 2, 3
+
+
+def tile_hebbianlayer_pb_w8_kernel(
+    tc, x_bytes, x_scale, w1_words, w1_scales, b1, w2_words, w2_scales, b2,
+    dopamine, serotonin, glutamate, gaba, out,
+):
+    nc = tc.nc
+    mods = {DOP: dopamine, SER: serotonin, GLU: glutamate, GAB: gaba}
+
+    with ExitStack() as ctx:
+        keep = ctx.enter_context(tc.tile_pool(name="keep", bufs=1))
+        work = ctx.enter_context(tc.tile_pool(name="work", bufs=2))
+        psum = ctx.enter_context(tc.psum_pool(name="psum", bufs=4))
+        ctx.enter_context(tc.manual_schedule())
+
+        def kt(shape, dtype, name):
+            return keep.tile(shape, dtype, name=name, align_bytes=64)
+
+        xb = kt([P, 4, D], U8, "xb")
+        xs = kt([P, 8], F32, "xs")
+        b1r = kt([P, 2, 4], BF16, "b1r")
+        b1c = kt([P, 8], F32, "b1c")
+        b2r = kt([P, 8, 4], BF16, "b2r")
+        b2c = kt([P, 8, 4], F32, "b2c")
+        w1r = kt([P, 2, D], I32, "w1r")
+        w1p = kt([P, 2, D], I32, "w1p")
+        w1s = kt([P, D], U8, "w1s")
+        w1sp = kt([P, D], U8, "w1sp")
+        w2r = [kt([P, 2, D], I32, f"w2r{q}") for q in range(4)]
+        w2p = kt([P, 2, NM, E], I32, "w2p")
+        w2s = kt([P, NM * 512], U8, "w2s")
+        w2sp = kt([P, NM, 512], U8, "w2sp")
+        mod = {c: kt([P, 4, E], BF16, f"mod{c}") for c in range(NM)}
+        ident = kt([P, P], F32, "ident")
+        dummy = kt([P, 1], F32, "dummy")
+        xg = kt([P, 2, B, 4], BF16, "xg")
+        xc = kt([P, 2, B], U32, "xc")
+        xsc = kt([P, 2, B], U8, "xsc")
+        hc = kt([P, 2, B], U32, "hc")
+        hsc = kt([P, 2, B], U8, "hsc")
+        s_sb = kt([P, 8, B], F32, "s_sb")
+        inv = kt([P, 8, B], F32, "inv")
+
+        xv = x_bytes.rearrange("(p i) k -> p i k", i=4)
+        nc.gpsimd.dma_start(out=xs[:], in_=x_scale.rearrange("o (g p t) -> p (o g) t", p=P, t=4))
+        nc.sync.dma_start(out=xb[:, 0:2, :], in_=xv[:, 0:2, :])
+        nc.vector.memset(dummy[:], 0.0)
+        nc.vector.memset(w1s[:].bitcast(I32), 0)
+        nc.vector.memset(w2s[:].bitcast(I32), 0)
+        nc.scalar.activation(out=dummy[:], in_=dummy[:], func=ACT.Tanh)
+        make_identity(nc, ident[:])
+        nc.gpsimd.dma_start(out=b1r[:], in_=b1.rearrange("(g m t) -> m g t", m=P, t=4))
+        nc.gpsimd.dma_start(out=b2r[:], in_=b2.rearrange("(u p c) -> p u c", p=P, c=4))
+        nc.sync.dma_start(out=w1r[:], in_=w1_words.rearrange("g p n t -> p g (n t)").bitcast(I32))
+        for q in range(4):
+            nc.sync.dma_start(
+                out=w1s[32 * q : 32 * q + 8, :].bitcast(I32),
+                in_=w1_scales[:, 4 * q : 4 * q + 4, :].bitcast(I32),
+            )
+        nc.sync.dma_start(out=xb[:, 2:4, :], in_=xv[:, 2:4, :])
+        w2v = w2_words.rearrange("g p n t -> p g (n t)")
+        for q in range(4):
+            nc.sync.dma_start(out=w2r[q][:], in_=w2v[:, :, 4096 * q : 4096 * (q + 1)].bitcast(I32))
+            if q == 0:
+                for r0 in range(0, P, 32):
+                    for s in range(2):
+                        nc.sync.dma_start(
+                            out=w2s[r0 + 8 * s : r0 + 8 * s + 8, :].bitcast(I32),
+                            in_=w2_scales[:, r0 // 8 : r0 // 8 + 4, 2048 * s : 2048 * (s + 1)].bitcast(I32),
+                        )
+        for c in (SER, DOP, GLU, GAB):
+            nc.sync.dma_start(out=mod[c][:], in_=mods[c].rearrange("(p i) u -> p i u", i=4))
+
+        xbf = [work.tile([P, D], BF16, name=f"xbf{i}", tag="xbf", bufs=4, align_bytes=64) for i in range(4)]
+
+        def cast_x(i, eng):
+            src = xb[:, i, :].bitcast(FP8)
+            if eng == "v":
+                nc.vector.tensor_copy(out=xbf[i][:], in_=src)
+            else:
+                nc.scalar.copy(out=xbf[i][:], in_=src)
+
+        xt = {}
+
+        def turn_x(i):
+            bank = psum.tile([P, 2, 2, P], F32, name=f"xt{i}", tag="tp")
+            words = xbf[i][:].bitcast(F32)
+            for g in range(2):
+                for u in range(2):
+                    nc.tensor.transpose(bank[:, g, u, :], words[:, 256 * g + u : 256 * (g + 1) : 2], ident[:])
+            xt[i] = bank
+
+        def scale_x(i, gs=(0, 1)):
+            for g in gs:
+                src = xt[i][:, g, :, :].rearrange("p u r -> p (u r)").bitcast(BF16)
+                sc = xs[:, 4 * g : 4 * g + 4].rearrange("p (u e) -> p u e", u=2).unsqueeze(1)
+                nc.vector.tensor_tensor(
+                    out=xg[:, g, P * i : P * (i + 1), :].rearrange("p r (u e) -> p r u e", u=2),
+                    in0=src.rearrange("p (u r e) -> p r u e", u=2, e=2),
+                    in1=sc.broadcast_to([P, P, 2, 2]),
+                    op=ALU.mult,
+                )
+
+        def quant_x(h):
+            tok = slice(256 * h, 256 * (h + 1))
+            for g in range(2):
+                nc.vector.quantize_mx(
+                    out=xc[:, g, tok].bitcast(FP8X4), scales=xsc[:, g, tok],
+                    in_=xg[:, g, tok, :].rearrange("p r t -> p (r t)"),
+                )
+
+        def perm_w1(gg):
+            cols = slice(512 * gg, 512 * (gg + 1))
+            nc.vector.tensor_copy(
+                out=w1p[:, :, cols].rearrange("p g (t m) -> p g m t", t=4),
+                in_=w1r[:, :, cols].rearrange("p g (m t) -> p g m t", t=4),
+            )
+
+        def perm_w1s(gg):
+            cols = slice(512 * gg, 512 * (gg + 1))
+            nc.vector.tensor_copy(
+                out=w1sp[:, cols].rearrange("p (t m) -> p m t", t=4),
+                in_=w1s[:, cols].rearrange("p (m t) -> p m t", t=4),
+            )
+
+        def perm_w2(c, q):
+            nc.vector.tensor_copy(
+                out=w2p[:, :, c, 256 * q : 256 * (q + 1)],
+                in_=w2r[q][:].rearrange("p g (u c) -> p g u c", c=4)[:, :, :, c],
+            )
+
+        def perm_w2s(c):
+            nc.vector.tensor_copy(out=w2sp[:, c, :], in_=w2s[:].rearrange("p (u c) -> p u c", c=4)[:, :, c])
+
+        l1 = {}
+
+        def mm_l1(h, gg):
+            tok = slice(256 * h, 256 * (h + 1))
+            for tt in range(2):
+                bank = psum.tile([P, 2, 256], F32, name=f"l1_{h}_{gg}_{tt}", tag="mx")
+                for k in range(2):
+                    c0 = 512 * gg + P * (2 * tt + k)
+                    for g in range(2):
+                        nc.tensor.matmul_mx(
+                            out=bank[:, k, :],
+                            lhsT=w1p[:, g, c0 : c0 + P].bitcast(FP8X4), lhsT_scale=w1sp[4 * g :, c0 : c0 + P],
+                            rhs=xc[:, g, tok].bitcast(FP8X4), rhs_scale=xsc[:, g, tok],
+                            start=(g == 0), stop=(g == 1),
+                        )
+                l1[h, gg, tt] = bank
+
+        hid = {}
+
+        def relu(h, gg, eng):
+            hid[h, gg] = work.tile([P, 4, 256], BF16, name=f"hid{h}{gg}", tag="hid", bufs=2, align_bytes=64)
+            for t in range(4):
+                src = l1[h, gg, t // 2][:, t % 2, :]
+                col = b1c[:, 4 * gg + t : 4 * gg + t + 1]
+                if eng == "s":
+                    nc.scalar.activation(out=hid[h, gg][:, t, :], in_=src, func=ACT.Relu, bias=col)
+                else:
+                    nc.vector.tensor_scalar(
+                        out=hid[h, gg][:, t, :], in0=src, scalar1=col, scalar2=0.0, op0=ALU.add, op1=ALU.max
+                    )
+
+        hg = {}
+
+        def lace(h, gg):
+            hg[h, gg] = work.tile([P, 256, 4], BF16, name=f"hg{h}{gg}", tag="hg", bufs=2, align_bytes=64)
+            nc.vector.tensor_copy(
+                out=hg[h, gg][:].rearrange("p (c i) t -> p c t i", i=4),
+                in_=hid[h, gg][:].rearrange("p t (c i) -> p c t i", i=4),
+            )
+
+        def quant_h(h, gg):
+            tok = slice(256 * h, 256 * (h + 1))
+            nc.vector.quantize_mx(
+                out=hc[:, gg, tok].bitcast(FP8X4), scales=hsc[:, gg, tok],
+                in_=hg[h, gg][:].rearrange("p r t -> p (r t)"),
+            )
+
+        def mm_l2(dst, c, ut, tok):
+            cols = slice(P * ut, P * (ut + 1))
+            for g in range(2):
+                nc.tensor.matmul_mx(
+                    out=dst,
+                    lhsT=w2p[:, g, c, cols].bitcast(FP8X4), lhsT_scale=w2sp[8 * (ut // 4) + 4 * g :, c, P * (ut % 4) : P * (ut % 4 + 1)],
+                    rhs=hc[:, g, tok].bitcast(FP8X4), rhs_scale=hsc[:, g, tok],
+                    start=(g == 0), stop=(g == 1),
+                )
+
+        banks = {}
+
+        def ser_mm(h, b):
+            tok = slice(256 * h, 256 * (h + 1))
+            bank = psum.tile([P, 2, 256], F32, name=f"ser{h}{b}", tag="mx")
+            for k in range(2):
+                mm_l2(bank[:, k, :], SER, 2 * b + k, tok)
+            banks[h, b] = bank
+
+        def ser_tanh(h, b):
+            tok = slice(256 * h, 256 * (h + 1))
+            bank = banks[h, b]
+            for k in range(2):
+                ut = 2 * b + k
+                nc.scalar.activation(
+                    out=s_sb[:, ut, tok], in_=bank[:, k, :], func=ACT.Tanh, bias=b2c[:, ut, SER : SER + 1]
+                )
+
+        def square(h, b, eng):
+            ut, tok = slice(2 * b, 2 * b + 2), slice(256 * h, 256 * (h + 1))
+            src = s_sb[:, ut, tok]
+            if eng == "s":
+                nc.scalar.activation(out=inv[:, ut, tok], in_=src, func=ACT.Square)
+            else:
+                e = nc.gpsimd if eng == "g" else nc.vector
+                e.tensor_tensor(out=inv[:, ut, tok], in0=src, in1=src, op=ALU.mult)
+
+        def clamp(h, b, eng):
+            ut, tok = slice(2 * b, 2 * b + 2), slice(256 * h, 256 * (h + 1))
+            if eng == "g":
+                nc.gpsimd.tensor_scalar(
+                    out=inv[:, ut, tok], in0=inv[:, ut, tok], scalar1=1e-12, scalar2=1.0, op0=ALU.max, op1=ALU.mult
+                )
+            else:
+                nc.vector.tensor_scalar_max(inv[:, ut, tok], inv[:, ut, tok], 1e-12)
+
+        def rsqrt(b):
+            ut = slice(2 * b, 2 * b + 2)
+            nc.scalar.activation(out=inv[:, ut, :], in_=inv[:, ut, :], func=ACT.Abs_reciprocal_sqrt)
+
+        pt = {}
+
+        def step_mm(c, uh):
+            for k in range(4):
+                bank = psum.tile([P, B], F32, name=f"mx{c}{uh}{k}", tag="mx")
+                mm_l2(bank[:], c, 4 * uh + k, slice(0, B))
+                banks[c, uh, k] = bank
+
+        def step_tanh(c, uh):
+            p = work.tile([P, 4, B], F32, name=f"p{c}{uh}", tag="p", bufs=3, align_bytes=64)
+            for k in range(4):
+                ut = 4 * uh + k
+                nc.scalar.activation(out=p[:, k, :], in_=banks[c, uh, k][:], func=ACT.Tanh, bias=b2c[:, ut, c : c + 1])
+            pt[c, uh] = p
+
+        def step_mul(c, uh, k, eng):
+            p = pt[c, uh]
+            (nc.gpsimd if eng == "g" else nc.vector).tensor_tensor(
+                out=p[:, k, :], in0=p[:, k, :], in1=inv[:, 4 * uh + k, :], op=ALU.mult
+            )
+
+        ov = out.rearrange("(c p i) u -> c p i u", c=4, i=4)
+
+        def step_out(c, uh):
+            src = s_sb[:, 4 * uh : 4 * uh + 4, :] if c == SER else pt[c, uh][:]
+            us = slice(512 * uh, 512 * (uh + 1))
+            for i in range(4):
+                o = work.tile([P, 512], F32, name=f"o{c}{uh}{i}", tag="o", bufs=8, align_bytes=64)
+                bank = psum.tile([P, 512], F32, name=f"t{c}{uh}{i}", tag="tp")
+                for k in range(4):
+                    nc.tensor.transpose(bank[:, P * k : P * (k + 1)], src[:, k, P * i : P * (i + 1)], ident[:])
+                nc.vector.tensor_tensor(out=o[:], in0=bank[:], in1=mod[c][:, i, us], op=ALU.add)
+                nc.sync.dma_start(out=ov[c, :, i, us], in_=o[:])
+
+        cast_x(0, "v")
+        cast_x(1, "s")
+        turn_x(0)
+        turn_x(1)
+        scale_x(0)
+        scale_x(1)
+        quant_x(0)
+        nc.vector.tensor_copy(out=b1c[:].rearrange("p (g t) -> p g t", t=4), in_=b1r[:])
+        perm_w1s(0)
+        perm_w1(0)
+        cast_x(2, "s")
+        cast_x(3, "s")
+        turn_x(2)
+        turn_x(3)
+        mm_l1(0, 0)
+        relu(0, 0, "s")
+        perm_w1s(1)
+        perm_w1(1)
+        mm_l1(0, 1)
+        relu(0, 1, "s")
+        scale_x(2)
+        scale_x(3)
+        quant_x(1)
+        mm_l1(1, 0)
+        relu(1, 0, "s")
+        lace(0, 0)
+        perm_w2s(SER)
+        quant_h(0, 0)
+        mm_l1(1, 1)
+        relu(1, 1, "s")
+        lace(0, 1)
+        perm_w2(SER, 0)
+        quant_h(0, 1)
+        perm_w2(SER, 1)
+        lace(1, 0)
+        perm_w2(SER, 2)
+        quant_h(1, 0)
+        nc.vector.tensor_copy(out=b2c[:], in_=b2r[:])
+        ser_mm(0, 0)
+        ser_tanh(0, 0)
+        ser_mm(0, 1)
+        ser_tanh(0, 1)
+        lace(1, 1)
+        perm_w2(SER, 3)
+        quant_h(1, 1)
+        ser_mm(0, 2)
+        ser_tanh(0, 2)
+        ser_mm(0, 3)
+        ser_tanh(0, 3)
+        perm_w2s(DOP)
+        for q in range(2):
+            perm_w2(DOP, q)
+        for b in range(4):
+            square(0, b, "v")
+        for b in range(4):
+            ser_mm(1, b)
+            ser_tanh(1, b)
+        for b in range(4):
+            clamp(0, b, "v")
+        for q in range(2, 4):
+            perm_w2(DOP, q)
+        for b in range(4):
+            square(1, b, "v")
+        for b in range(4):
+            clamp(1, b, "v")
+        step_mm(DOP, 0)
+        step_tanh(DOP, 0)
+        perm_w2s(GLU)
+        step_mm(DOP, 1)
+        step_tanh(DOP, 1)
+        for q in range(4):
+            perm_w2(GLU, q)
+        for b in range(4):
+            rsqrt(b)
+        step_out(SER, 0)
+        step_mm(GLU, 0)
+        steps = [(DOP, 0), (DOP, 1), (GLU, 0), (GLU, 1), (GAB, 0), (GAB, 1)]
+        pats = ["vgvg"]*6
+        for n in range(len(steps) + 1):
+            if n < len(steps):
+                for k in range(4):
+                    step_mul(*steps[n], k, pats[n][k])
+            if n == 0:
+                step_out(SER, 1)
+                perm_w2s(GAB)
+                for q in range(4):
+                    perm_w2(GAB, q)
+            if n >= 1:
+                step_out(*steps[n - 1])
+                if n + 2 < len(steps):
+                    step_mm(*steps[n + 2])
+            if n + 2 < len(steps):
+                step_tanh(*steps[n + 2])

@@ -45,12 +45,13 @@ def tile_hebbianlayer_pb_w8_kernel(
         w1p = kt([P, 2, D], I32, "w1p")
         w1s = kt([P, D], U8, "w1s")
         w1sp = kt([P, D], U8, "w1sp")
-        w2r = [kt([P, 2, D], I32, f"w2r{q}") for q in range(4)]
+        w2r = kt([P, 4, 2, D], I32, "w2r")
         w2p = kt([P, 2, NM, E], I32, "w2p")
         w2s = kt([P, NM * 512], U8, "w2s")
         w2sp = kt([P, NM, 512], U8, "w2sp")
         mod = {c: kt([P, 4, E], BF16, f"mod{c}") for c in range(NM)}
         ident = kt([P, P], F32, "ident")
+        ident16 = kt([P, P], BF16, "ident16")
         dummy = kt([P, 1], F32, "dummy")
         xg = kt([P, 2, B, 4], BF16, "xg")
         xc = kt([P, 2, B], U32, "xc")
@@ -61,32 +62,33 @@ def tile_hebbianlayer_pb_w8_kernel(
         inv = kt([P, 8, B], F32, "inv")
 
         xv = x_bytes.rearrange("(p i) k -> p i k", i=4)
-        nc.gpsimd.dma_start(out=xs[:], in_=x_scale.rearrange("o (g p t) -> p (o g) t", p=P, t=4))
+        nc.scalar.dma_start(out=xs[:], in_=x_scale.rearrange("o (g p t) -> p (o g) t", p=P, t=4))
         nc.sync.dma_start(out=xb[:, 0:2, :], in_=xv[:, 0:2, :])
+        nc.scalar.dma_start(out=b1r[:], in_=b1.rearrange("(g m t) -> m g t", m=P, t=4))
         nc.vector.memset(dummy[:], 0.0)
         nc.vector.memset(w1s[:].bitcast(I32), 0)
         nc.vector.memset(w2s[:].bitcast(I32), 0)
         nc.scalar.activation(out=dummy[:], in_=dummy[:], func=ACT.Tanh)
         make_identity(nc, ident[:])
-        nc.gpsimd.dma_start(out=b1r[:], in_=b1.rearrange("(g m t) -> m g t", m=P, t=4))
-        nc.gpsimd.dma_start(out=b2r[:], in_=b2.rearrange("(u p c) -> p u c", p=P, c=4))
+        nc.gpsimd.tensor_copy(out=ident16[:], in_=ident[:])
+        nc.gpsimd.tensor_copy(out=b1c[:].rearrange("p (g t) -> p g t", t=4), in_=b1r[:])
         nc.sync.dma_start(out=w1r[:], in_=w1_words.rearrange("g p n t -> p g (n t)").bitcast(I32))
-        for q in range(4):
-            nc.sync.dma_start(
-                out=w1s[32 * q : 32 * q + 8, :].bitcast(I32),
-                in_=w1_scales[:, 4 * q : 4 * q + 4, :].bitcast(I32),
-            )
         nc.sync.dma_start(out=xb[:, 2:4, :], in_=xv[:, 2:4, :])
+        for r0 in range(0, P, 32):
+            nc.sync.dma_start(
+                out=w1s[r0 : r0 + 8, :].bitcast(I32), in_=w1_scales[:, r0 // 8 : r0 // 8 + 4, :].bitcast(I32)
+            )
+        for r0 in range(0, P, 32):
+            for s in range(2):
+                nc.sync.dma_start(
+                    out=w2s[r0 + 8 * s : r0 + 8 * s + 8, :].bitcast(I32),
+                    in_=w2_scales[:, r0 // 8 : r0 // 8 + 4, 2048 * s : 2048 * (s + 1)].bitcast(I32),
+                )
+        nc.gpsimd.dma_start(out=b2r[:], in_=b2.rearrange("(u p c) -> p u c", p=P, c=4))
+        nc.gpsimd.tensor_copy(out=b2c[:], in_=b2r[:])
         w2v = w2_words.rearrange("g p n t -> p g (n t)")
         for q in range(4):
-            nc.sync.dma_start(out=w2r[q][:], in_=w2v[:, :, 4096 * q : 4096 * (q + 1)].bitcast(I32))
-            if q == 0:
-                for r0 in range(0, P, 32):
-                    for s in range(2):
-                        nc.sync.dma_start(
-                            out=w2s[r0 + 8 * s : r0 + 8 * s + 8, :].bitcast(I32),
-                            in_=w2_scales[:, r0 // 8 : r0 // 8 + 4, 2048 * s : 2048 * (s + 1)].bitcast(I32),
-                        )
+            nc.sync.dma_start(out=w2r[:, q], in_=w2v[:, :, 4096 * q : 4096 * (q + 1)].bitcast(I32))
         for c in (SER, DOP, GLU, GAB):
             nc.sync.dma_start(out=mod[c][:], in_=mods[c].rearrange("(p i) u -> p i u", i=4))
 
@@ -109,16 +111,19 @@ def tile_hebbianlayer_pb_w8_kernel(
                     nc.tensor.transpose(bank[:, g, u, :], words[:, 256 * g + u : 256 * (g + 1) : 2], ident[:])
             xt[i] = bank
 
-        def scale_x(i, gs=(0, 1)):
-            for g in gs:
-                src = xt[i][:, g, :, :].rearrange("p u r -> p (u r)").bitcast(BF16)
-                sc = xs[:, 4 * g : 4 * g + 4].rearrange("p (u e) -> p u e", u=2).unsqueeze(1)
-                nc.vector.tensor_tensor(
-                    out=xg[:, g, P * i : P * (i + 1), :].rearrange("p r (u e) -> p r u e", u=2),
-                    in0=src.rearrange("p (u r e) -> p r u e", u=2, e=2),
-                    in1=sc.broadcast_to([P, P, 2, 2]),
-                    op=ALU.mult,
-                )
+        def scale_x(i, g, eng):
+            bank = xt[i][:, g, :, :].rearrange("p u r -> p (u r)")
+            if eng == "g":
+                half = work.tile([P, 256], F32, name=f"half{i}{g}", tag="half", bufs=2, align_bytes=64)
+                nc.scalar.copy(out=half[:], in_=bank)
+                bank = half[:]
+            sc = xs[:, 4 * g : 4 * g + 4].rearrange("p (u e) -> p u e", u=2).unsqueeze(1)
+            (nc.gpsimd if eng == "g" else nc.vector).tensor_tensor(
+                out=xg[:, g, P * i : P * (i + 1), :].rearrange("p r (u e) -> p r u e", u=2),
+                in0=bank.bitcast(BF16).rearrange("p (u r e) -> p r u e", u=2, e=2),
+                in1=sc.broadcast_to([P, P, 2, 2]),
+                op=ALU.mult,
+            )
 
         def quant_x(h):
             tok = slice(256 * h, 256 * (h + 1))
@@ -142,14 +147,19 @@ def tile_hebbianlayer_pb_w8_kernel(
                 in_=w1s[:, cols].rearrange("p (m t) -> p m t", t=4),
             )
 
-        def perm_w2(c, q):
+        def perm_w2(half, q):
+            cs = slice(2 * half, 2 * half + 2)
             nc.vector.tensor_copy(
-                out=w2p[:, :, c, 256 * q : 256 * (q + 1)],
-                in_=w2r[q][:].rearrange("p g (u c) -> p g u c", c=4)[:, :, :, c],
+                out=w2p[:, :, cs, 256 * q : 256 * (q + 1)].rearrange("p g c u -> p g u c"),
+                in_=w2r[:, q].rearrange("p g (u c) -> p g u c", c=4)[:, :, :, cs],
             )
 
-        def perm_w2s(c):
-            nc.vector.tensor_copy(out=w2sp[:, c, :], in_=w2s[:].rearrange("p (u c) -> p u c", c=4)[:, :, c])
+        def perm_w2s(half):
+            cs = slice(2 * half, 2 * half + 2)
+            nc.vector.tensor_copy(
+                out=w2sp[:, cs, :].rearrange("p c u -> p u c"),
+                in_=w2s[:].rearrange("p (u c) -> p u c", c=4)[:, :, cs],
+            )
 
         l1 = {}
 
@@ -184,9 +194,9 @@ def tile_hebbianlayer_pb_w8_kernel(
 
         hg = {}
 
-        def lace(h, gg):
+        def lace(h, gg, eng):
             hg[h, gg] = work.tile([P, 256, 4], BF16, name=f"hg{h}{gg}", tag="hg", bufs=2, align_bytes=64)
-            nc.vector.tensor_copy(
+            (nc.scalar.copy if eng == "s" else nc.vector.tensor_copy)(
                 out=hg[h, gg][:].rearrange("p (c i) t -> p c t i", i=4),
                 in_=hid[h, gg][:].rearrange("p t (c i) -> p c t i", i=4),
             )
@@ -226,8 +236,8 @@ def tile_hebbianlayer_pb_w8_kernel(
                     out=s_sb[:, ut, tok], in_=bank[:, k, :], func=ACT.Tanh, bias=b2c[:, ut, SER : SER + 1]
                 )
 
-        def square(h, b, eng):
-            ut, tok = slice(2 * b, 2 * b + 2), slice(256 * h, 256 * (h + 1))
+        def square(h, b0, b1, eng):
+            ut, tok = slice(2 * b0, 2 * b1), slice(256 * h, 256 * (h + 1))
             src = s_sb[:, ut, tok]
             if eng == "s":
                 nc.scalar.activation(out=inv[:, ut, tok], in_=src, func=ACT.Square)
@@ -235,14 +245,12 @@ def tile_hebbianlayer_pb_w8_kernel(
                 e = nc.gpsimd if eng == "g" else nc.vector
                 e.tensor_tensor(out=inv[:, ut, tok], in0=src, in1=src, op=ALU.mult)
 
-        def clamp(h, b, eng):
-            ut, tok = slice(2 * b, 2 * b + 2), slice(256 * h, 256 * (h + 1))
+        def clamp(h, eng):
+            z = inv[:, 2::4, 256 * h : 256 * (h + 1)]
             if eng == "g":
-                nc.gpsimd.tensor_scalar(
-                    out=inv[:, ut, tok], in0=inv[:, ut, tok], scalar1=1e-12, scalar2=1.0, op0=ALU.max, op1=ALU.mult
-                )
+                nc.gpsimd.tensor_scalar(out=z, in0=z, scalar1=1e-12, scalar2=1.0, op0=ALU.max, op1=ALU.mult)
             else:
-                nc.vector.tensor_scalar_max(inv[:, ut, tok], inv[:, ut, tok], 1e-12)
+                nc.vector.tensor_scalar_max(z, z, 1e-12)
 
         def rsqrt(b):
             ut = slice(2 * b, 2 * b + 2)
@@ -250,128 +258,133 @@ def tile_hebbianlayer_pb_w8_kernel(
 
         pt = {}
 
-        def step_mm(c, uh):
-            for k in range(4):
-                bank = psum.tile([P, B], F32, name=f"mx{c}{uh}{k}", tag="mx")
-                mm_l2(bank[:], c, 4 * uh + k, slice(0, B))
-                banks[c, uh, k] = bank
+        def step_mm(c, uh, k):
+            bank = psum.tile([P, B], F32, name=f"mx{c}{uh}{k}", tag="mx")
+            mm_l2(bank[:], c, 4 * uh + k, slice(0, B))
+            banks[c, uh, k] = bank
 
-        def step_tanh(c, uh):
-            p = work.tile([P, 4, B], F32, name=f"p{c}{uh}", tag="p", bufs=3, align_bytes=64)
-            for k in range(4):
-                ut = 4 * uh + k
-                nc.scalar.activation(out=p[:, k, :], in_=banks[c, uh, k][:], func=ACT.Tanh, bias=b2c[:, ut, c : c + 1])
-            pt[c, uh] = p
-
-        def step_mul(c, uh, k, eng):
-            p = pt[c, uh]
-            (nc.gpsimd if eng == "g" else nc.vector).tensor_tensor(
-                out=p[:, k, :], in0=p[:, k, :], in1=inv[:, 4 * uh + k, :], op=ALU.mult
+        def step_tanh(c, uh, k):
+            if k == 0:
+                pt[c, uh] = work.tile([P, 4, B], F32, name=f"p{c}{uh}", tag="p", bufs=3, align_bytes=64)
+            ut = 4 * uh + k
+            nc.scalar.activation(
+                out=pt[c, uh][:, k, :], in_=banks[c, uh, k][:], func=ACT.Tanh, bias=b2c[:, ut, c : c + 1]
             )
+
+        def step_mul(c, uh, k0, k1, eng):
+            p = pt[c, uh][:, k0:k1, :]
+            r = inv[:, 4 * uh + k0 : 4 * uh + k1, :]
+            if eng == "g":
+                nc.gpsimd.tensor_tensor(out=p, in0=p, in1=r, op=ALU.mult)
+            else:
+                nc.vector.scalar_tensor_tensor(out=p, in0=r, scalar=1e6, in1=p, op0=ALU.min, op1=ALU.mult)
 
         ov = out.rearrange("(c p i) u -> c p i u", c=4, i=4)
 
-        def step_out(c, uh):
+        def step_tr(c, uh, i, eng):
             src = s_sb[:, 4 * uh : 4 * uh + 4, :] if c == SER else pt[c, uh][:]
             us = slice(512 * uh, 512 * (uh + 1))
-            for i in range(4):
-                o = work.tile([P, 512], F32, name=f"o{c}{uh}{i}", tag="o", bufs=8, align_bytes=64)
-                bank = psum.tile([P, 512], F32, name=f"t{c}{uh}{i}", tag="tp")
+            o = work.tile([P, 512], F32, name=f"o{c}{uh}{i}", tag="o", bufs=8, align_bytes=64)
+            bank = psum.tile([P, 512], F32, name=f"t{c}{uh}{i}", tag="tp")
+            if eng == "s":
+                nc.tensor.matmul(bank[:], lhsT=ident16[:], rhs=mod[c][:, i, us], start=True, stop=False)
+                for k in range(4):
+                    nc.tensor.matmul(
+                        bank[:, P * k : P * (k + 1)], lhsT=src[:, k, P * i : P * (i + 1)], rhs=ident[:],
+                        is_transpose=True, start=False, stop=(k == 3),
+                    )
+                nc.scalar.copy(out=o[:], in_=bank[:])
+            else:
                 for k in range(4):
                     nc.tensor.transpose(bank[:, P * k : P * (k + 1)], src[:, k, P * i : P * (i + 1)], ident[:])
                 nc.vector.tensor_tensor(out=o[:], in0=bank[:], in1=mod[c][:, i, us], op=ALU.add)
-                nc.sync.dma_start(out=ov[c, :, i, us], in_=o[:])
+            nc.sync.dma_start(out=ov[c, :, i, us], in_=o[:])
 
         cast_x(0, "v")
         cast_x(1, "s")
         turn_x(0)
         turn_x(1)
-        scale_x(0)
-        scale_x(1)
-        quant_x(0)
-        nc.vector.tensor_copy(out=b1c[:].rearrange("p (g t) -> p g t", t=4), in_=b1r[:])
-        perm_w1s(0)
+        scale_x(0, 0, "v")
+        scale_x(0, 1, "v")
         perm_w1(0)
+        scale_x(1, 0, "v")
+        scale_x(1, 1, "v")
+        perm_w1s(0)
+        quant_x(0)
         cast_x(2, "s")
         cast_x(3, "s")
         turn_x(2)
         turn_x(3)
+        perm_w1(1)
+        perm_w1s(1)
         mm_l1(0, 0)
         relu(0, 0, "s")
-        perm_w1s(1)
-        perm_w1(1)
+        lace(0, 0, "s")
         mm_l1(0, 1)
         relu(0, 1, "s")
-        scale_x(2)
-        scale_x(3)
+        for i in range(2, 4):
+            scale_x(i, 0, "v")
+            scale_x(i, 1, "v")
         quant_x(1)
         mm_l1(1, 0)
         relu(1, 0, "s")
-        lace(0, 0)
-        perm_w2s(SER)
-        quant_h(0, 0)
         mm_l1(1, 1)
         relu(1, 1, "s")
-        lace(0, 1)
-        perm_w2(SER, 0)
+        perm_w2s(0)
+        perm_w2(0, 0)
+        lace(0, 1, "v")
+        quant_h(0, 0)
         quant_h(0, 1)
-        perm_w2(SER, 1)
-        lace(1, 0)
-        perm_w2(SER, 2)
-        quant_h(1, 0)
-        nc.vector.tensor_copy(out=b2c[:], in_=b2r[:])
         ser_mm(0, 0)
         ser_tanh(0, 0)
+        perm_w2(0, 1)
         ser_mm(0, 1)
         ser_tanh(0, 1)
-        lace(1, 1)
-        perm_w2(SER, 3)
-        quant_h(1, 1)
+        lace(1, 0, "v")
+        lace(1, 1, "v")
+        perm_w2(0, 2)
         ser_mm(0, 2)
         ser_tanh(0, 2)
+        quant_h(1, 0)
+        perm_w2(0, 3)
         ser_mm(0, 3)
         ser_tanh(0, 3)
-        perm_w2s(DOP)
-        for q in range(2):
-            perm_w2(DOP, q)
-        for b in range(4):
-            square(0, b, "v")
+        quant_h(1, 1)
         for b in range(4):
             ser_mm(1, b)
             ser_tanh(1, b)
-        for b in range(4):
-            clamp(0, b, "v")
-        for q in range(2, 4):
-            perm_w2(DOP, q)
-        for b in range(4):
-            square(1, b, "v")
-        for b in range(4):
-            clamp(1, b, "v")
-        step_mm(DOP, 0)
-        step_tanh(DOP, 0)
-        perm_w2s(GLU)
-        step_mm(DOP, 1)
-        step_tanh(DOP, 1)
-        for q in range(4):
-            perm_w2(GLU, q)
+
+        square(0, 0, 2, "v")
+        square(0, 2, 4, "v")
+        perm_w2s(1)
+        perm_w2(1, 0)
+        perm_w2(1, 1)
+        square(1, 0, 2, "v")
+        perm_w2(1, 2)
+        square(1, 2, 4, "v")
+        perm_w2(1, 3)
+        for uh in range(2):
+            for k in range(4):
+                step_mm(DOP, uh, k)
+                step_tanh(DOP, uh, k)
         for b in range(4):
             rsqrt(b)
-        step_out(SER, 0)
-        step_mm(GLU, 0)
+        for uh in range(2):
+            for i in range(4):
+                step_tr(SER, uh, i, "v")
+        for k in range(4):
+            step_mm(GLU, 0, k)
         steps = [(DOP, 0), (DOP, 1), (GLU, 0), (GLU, 1), (GAB, 0), (GAB, 1)]
-        pats = ["vgvg"]*6
         for n in range(len(steps) + 1):
             if n < len(steps):
                 for k in range(4):
-                    step_mul(*steps[n], k, pats[n][k])
-            if n == 0:
-                step_out(SER, 1)
-                perm_w2s(GAB)
-                for q in range(4):
-                    perm_w2(GAB, q)
+                    step_mul(*steps[n], k, k + 1, "v")
             if n >= 1:
-                step_out(*steps[n - 1])
+                for i in range(4):
+                    step_tr(*steps[n - 1], i, "vsvs"[i])
                 if n + 2 < len(steps):
-                    step_mm(*steps[n + 2])
+                    for k in range(4):
+                        step_mm(*steps[n + 2], k)
             if n + 2 < len(steps):
-                step_tanh(*steps[n + 2])
+                for k in range(4):
+                    step_tanh(*steps[n + 2], k)

from contextlib import ExitStack

import concourse.mybir as mybir
from concourse.masks import make_identity

F32 = mybir.dt.float32
BF16 = mybir.dt.bfloat16
I32 = mybir.dt.int32
U32 = mybir.dt.uint32
U8 = mybir.dt.uint8
FP8 = mybir.dt.float8_e4m3fn
FP8X4 = mybir.dt.float8_e4m3fn_x4
ACT = mybir.ActivationFunctionType
ALU = mybir.AluOpType

P = 128
B, D, E, NM = 512, 1024, 1024, 4
FLOPS = 2 * B * D * D + 2 * B * D * NM * E
DOP, SER, GLU, GAB = 0, 1, 2, 3


def tile_hebbianlayer_pb_w8_kernel(
    tc, x_bytes, x_scale, w1_words, w1_scales, b1, w2_words, w2_scales, b2,
    dopamine, serotonin, glutamate, gaba, out,
):
    nc = tc.nc
    mods = {DOP: dopamine, SER: serotonin, GLU: glutamate, GAB: gaba}

    with ExitStack() as ctx:
        keep = ctx.enter_context(tc.tile_pool(name="keep", bufs=1))
        work = ctx.enter_context(tc.tile_pool(name="work", bufs=2))
        psum = ctx.enter_context(tc.psum_pool(name="psum", bufs=4))
        ctx.enter_context(tc.manual_schedule())

        def kt(shape, dtype, name):
            return keep.tile(shape, dtype, name=name, align_bytes=64)

        xb = kt([P, 4, D], U8, "xb")
        xs = kt([P, 8], F32, "xs")
        b1r = kt([P, 2, 4], BF16, "b1r")
        b1c = kt([P, 8], F32, "b1c")
        b2r = kt([P, 8, 4], BF16, "b2r")
        b2c = kt([P, 8, 4], F32, "b2c")
        w1r = kt([P, 2, D], I32, "w1r")
        w1p = kt([P, 2, D], I32, "w1p")
        w1s = kt([P, D], U8, "w1s")
        w1sp = kt([P, D], U8, "w1sp")
        w2r = kt([P, 4, 2, D], I32, "w2r")
        w2p = kt([P, 2, NM, E], I32, "w2p")
        w2s = kt([P, NM * 512], U8, "w2s")
        w2sp = kt([P, NM, 512], U8, "w2sp")
        mod = {c: kt([P, 4, E], BF16, f"mod{c}") for c in range(NM)}
        ident = kt([P, P], F32, "ident")
        ident16 = kt([P, P], BF16, "ident16")
        dummy = kt([P, 1], F32, "dummy")
        xg = kt([P, 2, B, 4], BF16, "xg")
        xc = kt([P, 2, B], U32, "xc")
        xsc = kt([P, 2, B], U8, "xsc")
        hc = kt([P, 2, B], U32, "hc")
        hsc = kt([P, 2, B], U8, "hsc")
        s_sb = kt([P, 8, B], F32, "s_sb")
        inv = kt([P, 8, B], F32, "inv")

        xv = x_bytes.rearrange("(p i) k -> p i k", i=4)
        nc.scalar.dma_start(out=xs[:], in_=x_scale.rearrange("o (g p t) -> p (o g) t", p=P, t=4))
        nc.sync.dma_start(out=xb[:, 0:2, :], in_=xv[:, 0:2, :])
        nc.scalar.dma_start(out=b1r[:], in_=b1.rearrange("(g m t) -> m g t", m=P, t=4))
        nc.vector.memset(dummy[:], 0.0)
        nc.vector.memset(w1s[:].bitcast(I32), 0)
        nc.vector.memset(w2s[:].bitcast(I32), 0)
        nc.scalar.activation(out=dummy[:], in_=dummy[:], func=ACT.Tanh)
        make_identity(nc, ident[:])
        nc.gpsimd.tensor_copy(out=ident16[:], in_=ident[:])
        nc.gpsimd.tensor_copy(out=b1c[:].rearrange("p (g t) -> p g t", t=4), in_=b1r[:])
        nc.sync.dma_start(out=w1r[:], in_=w1_words.rearrange("g p n t -> p g (n t)").bitcast(I32))
        nc.sync.dma_start(out=xb[:, 2:4, :], in_=xv[:, 2:4, :])
        for r0 in range(0, P, 32):
            nc.sync.dma_start(
                out=w1s[r0 : r0 + 8, :].bitcast(I32), in_=w1_scales[:, r0 // 8 : r0 // 8 + 4, :].bitcast(I32)
            )
        for r0 in range(0, P, 32):
            for s in range(2):
                nc.sync.dma_start(
                    out=w2s[r0 + 8 * s : r0 + 8 * s + 8, :].bitcast(I32),
                    in_=w2_scales[:, r0 // 8 : r0 // 8 + 4, 2048 * s : 2048 * (s + 1)].bitcast(I32),
                )
        nc.gpsimd.dma_start(out=b2r[:], in_=b2.rearrange("(u p c) -> p u c", p=P, c=4))
        nc.gpsimd.tensor_copy(out=b2c[:], in_=b2r[:])
        w2v = w2_words.rearrange("g p n t -> p g (n t)")
        for q in range(4):
            nc.sync.dma_start(out=w2r[:, q], in_=w2v[:, :, 4096 * q : 4096 * (q + 1)].bitcast(I32))
        for c in (SER, DOP, GLU, GAB):
            nc.sync.dma_start(out=mod[c][:], in_=mods[c].rearrange("(p i) u -> p i u", i=4))

        xbf = [work.tile([P, D], BF16, name=f"xbf{i}", tag="xbf", bufs=4, align_bytes=64) for i in range(4)]

        def cast_x(i, eng):
            src = xb[:, i, :].bitcast(FP8)
            if eng == "v":
                nc.vector.tensor_copy(out=xbf[i][:], in_=src)
            else:
                nc.scalar.copy(out=xbf[i][:], in_=src)

        xt = {}

        def turn_x(i):
            bank = psum.tile([P, 2, 2, P], F32, name=f"xt{i}", tag="tp")
            words = xbf[i][:].bitcast(F32)
            for g in range(2):
                for u in range(2):
                    nc.tensor.transpose(bank[:, g, u, :], words[:, 256 * g + u : 256 * (g + 1) : 2], ident[:])
            xt[i] = bank

        def scale_x(i, g, eng):
            bank = xt[i][:, g, :, :].rearrange("p u r -> p (u r)")
            if eng == "g":
                half = work.tile([P, 256], F32, name=f"half{i}{g}", tag="half", bufs=2, align_bytes=64)
                nc.scalar.copy(out=half[:], in_=bank)
                bank = half[:]
            sc = xs[:, 4 * g : 4 * g + 4].rearrange("p (u e) -> p u e", u=2).unsqueeze(1)
            (nc.gpsimd if eng == "g" else nc.vector).tensor_tensor(
                out=xg[:, g, P * i : P * (i + 1), :].rearrange("p r (u e) -> p r u e", u=2),
                in0=bank.bitcast(BF16).rearrange("p (u r e) -> p r u e", u=2, e=2),
                in1=sc.broadcast_to([P, P, 2, 2]),
                op=ALU.mult,
            )

        def quant_x(h):
            tok = slice(256 * h, 256 * (h + 1))
            for g in range(2):
                nc.vector.quantize_mx(
                    out=xc[:, g, tok].bitcast(FP8X4), scales=xsc[:, g, tok],
                    in_=xg[:, g, tok, :].rearrange("p r t -> p (r t)"),
                )

        def perm_w1(gg):
            cols = slice(512 * gg, 512 * (gg + 1))
            nc.vector.tensor_copy(
                out=w1p[:, :, cols].rearrange("p g (t m) -> p g m t", t=4),
                in_=w1r[:, :, cols].rearrange("p g (m t) -> p g m t", t=4),
            )

        def perm_w1s(gg):
            cols = slice(512 * gg, 512 * (gg + 1))
            nc.vector.tensor_copy(
                out=w1sp[:, cols].rearrange("p (t m) -> p m t", t=4),
                in_=w1s[:, cols].rearrange("p (m t) -> p m t", t=4),
            )

        def perm_w2(half, q):
            cs = slice(2 * half, 2 * half + 2)
            nc.vector.tensor_copy(
                out=w2p[:, :, cs, 256 * q : 256 * (q + 1)].rearrange("p g c u -> p g u c"),
                in_=w2r[:, q].rearrange("p g (u c) -> p g u c", c=4)[:, :, :, cs],
            )

        def perm_w2s(half):
            cs = slice(2 * half, 2 * half + 2)
            nc.vector.tensor_copy(
                out=w2sp[:, cs, :].rearrange("p c u -> p u c"),
                in_=w2s[:].rearrange("p (u c) -> p u c", c=4)[:, :, cs],
            )

        l1 = {}

        def mm_l1(h, gg):
            tok = slice(256 * h, 256 * (h + 1))
            for tt in range(2):
                bank = psum.tile([P, 2, 256], F32, name=f"l1_{h}_{gg}_{tt}", tag="mx")
                for k in range(2):
                    c0 = 512 * gg + P * (2 * tt + k)
                    for g in range(2):
                        nc.tensor.matmul_mx(
                            out=bank[:, k, :],
                            lhsT=w1p[:, g, c0 : c0 + P].bitcast(FP8X4), lhsT_scale=w1sp[4 * g :, c0 : c0 + P],
                            rhs=xc[:, g, tok].bitcast(FP8X4), rhs_scale=xsc[:, g, tok],
                            start=(g == 0), stop=(g == 1),
                        )
                l1[h, gg, tt] = bank

        hid = {}

        def relu(h, gg, eng):
            hid[h, gg] = work.tile([P, 4, 256], BF16, name=f"hid{h}{gg}", tag="hid", bufs=2, align_bytes=64)
            for t in range(4):
                src = l1[h, gg, t // 2][:, t % 2, :]
                col = b1c[:, 4 * gg + t : 4 * gg + t + 1]
                if eng == "s":
                    nc.scalar.activation(out=hid[h, gg][:, t, :], in_=src, func=ACT.Relu, bias=col)
                else:
                    nc.vector.tensor_scalar(
                        out=hid[h, gg][:, t, :], in0=src, scalar1=col, scalar2=0.0, op0=ALU.add, op1=ALU.max
                    )

        hg = {}

        def lace(h, gg, eng):
            hg[h, gg] = work.tile([P, 256, 4], BF16, name=f"hg{h}{gg}", tag="hg", bufs=2, align_bytes=64)
            (nc.scalar.copy if eng == "s" else nc.vector.tensor_copy)(
                out=hg[h, gg][:].rearrange("p (c i) t -> p c t i", i=4),
                in_=hid[h, gg][:].rearrange("p t (c i) -> p c t i", i=4),
            )

        def quant_h(h, gg):
            tok = slice(256 * h, 256 * (h + 1))
            nc.vector.quantize_mx(
                out=hc[:, gg, tok].bitcast(FP8X4), scales=hsc[:, gg, tok],
                in_=hg[h, gg][:].rearrange("p r t -> p (r t)"),
            )

        def mm_l2(dst, c, ut, tok):
            cols = slice(P * ut, P * (ut + 1))
            for g in range(2):
                nc.tensor.matmul_mx(
                    out=dst,
                    lhsT=w2p[:, g, c, cols].bitcast(FP8X4), lhsT_scale=w2sp[8 * (ut // 4) + 4 * g :, c, P * (ut % 4) : P * (ut % 4 + 1)],
                    rhs=hc[:, g, tok].bitcast(FP8X4), rhs_scale=hsc[:, g, tok],
                    start=(g == 0), stop=(g == 1),
                )

        banks = {}

        def ser_mm(h, b):
            tok = slice(256 * h, 256 * (h + 1))
            bank = psum.tile([P, 2, 256], F32, name=f"ser{h}{b}", tag="mx")
            for k in range(2):
                mm_l2(bank[:, k, :], SER, 2 * b + k, tok)
            banks[h, b] = bank

        def ser_tanh(h, b):
            tok = slice(256 * h, 256 * (h + 1))
            bank = banks[h, b]
            for k in range(2):
                ut = 2 * b + k
                nc.scalar.activation(
                    out=s_sb[:, ut, tok], in_=bank[:, k, :], func=ACT.Tanh, bias=b2c[:, ut, SER : SER + 1]
                )

        def square(h, b0, b1, eng):
            ut, tok = slice(2 * b0, 2 * b1), slice(256 * h, 256 * (h + 1))
            src = s_sb[:, ut, tok]
            if eng == "s":
                nc.scalar.activation(out=inv[:, ut, tok], in_=src, func=ACT.Square)
            else:
                e = nc.gpsimd if eng == "g" else nc.vector
                e.tensor_tensor(out=inv[:, ut, tok], in0=src, in1=src, op=ALU.mult)

        def clamp(h, eng):
            z = inv[:, 2::4, 256 * h : 256 * (h + 1)]
            if eng == "g":
                nc.gpsimd.tensor_scalar(out=z, in0=z, scalar1=1e-12, scalar2=1.0, op0=ALU.max, op1=ALU.mult)
            else:
                nc.vector.tensor_scalar_max(z, z, 1e-12)

        def rsqrt(b):
            ut = slice(2 * b, 2 * b + 2)
            nc.scalar.activation(out=inv[:, ut, :], in_=inv[:, ut, :], func=ACT.Abs_reciprocal_sqrt)

        pt = {}

        def step_mm(c, uh, k):
            bank = psum.tile([P, B], F32, name=f"mx{c}{uh}{k}", tag="mx")
            mm_l2(bank[:], c, 4 * uh + k, slice(0, B))
            banks[c, uh, k] = bank

        def step_tanh(c, uh, k):
            if k == 0:
                pt[c, uh] = work.tile([P, 4, B], F32, name=f"p{c}{uh}", tag="p", bufs=3, align_bytes=64)
            ut = 4 * uh + k
            nc.scalar.activation(
                out=pt[c, uh][:, k, :], in_=banks[c, uh, k][:], func=ACT.Tanh, bias=b2c[:, ut, c : c + 1]
            )

        def step_mul(c, uh, k0, k1, eng):
            p = pt[c, uh][:, k0:k1, :]
            r = inv[:, 4 * uh + k0 : 4 * uh + k1, :]
            if eng == "g":
                nc.gpsimd.tensor_tensor(out=p, in0=p, in1=r, op=ALU.mult)
            else:
                nc.vector.scalar_tensor_tensor(out=p, in0=r, scalar=1e6, in1=p, op0=ALU.min, op1=ALU.mult)

        ov = out.rearrange("(c p i) u -> c p i u", c=4, i=4)

        def step_tr(c, uh, i, eng):
            src = s_sb[:, 4 * uh : 4 * uh + 4, :] if c == SER else pt[c, uh][:]
            us = slice(512 * uh, 512 * (uh + 1))
            o = work.tile([P, 512], F32, name=f"o{c}{uh}{i}", tag="o", bufs=8, align_bytes=64)
            bank = psum.tile([P, 512], F32, name=f"t{c}{uh}{i}", tag="tp")
            if eng == "s":
                nc.tensor.matmul(bank[:], lhsT=ident16[:], rhs=mod[c][:, i, us], start=True, stop=False)
                for k in range(4):
                    nc.tensor.matmul(
                        bank[:, P * k : P * (k + 1)], lhsT=src[:, k, P * i : P * (i + 1)], rhs=ident[:],
                        is_transpose=True, start=False, stop=(k == 3),
                    )
                nc.scalar.copy(out=o[:], in_=bank[:])
            else:
                for k in range(4):
                    nc.tensor.transpose(bank[:, P * k : P * (k + 1)], src[:, k, P * i : P * (i + 1)], ident[:])
                nc.vector.tensor_tensor(out=o[:], in0=bank[:], in1=mod[c][:, i, us], op=ALU.add)
            nc.sync.dma_start(out=ov[c, :, i, us], in_=o[:])

        cast_x(0, "v")
        cast_x(1, "s")
        turn_x(0)
        turn_x(1)
        scale_x(0, 0, "v")
        scale_x(0, 1, "v")
        perm_w1(0)
        scale_x(1, 0, "v")
        scale_x(1, 1, "v")
        perm_w1s(0)
        quant_x(0)
        cast_x(2, "s")
        cast_x(3, "s")
        turn_x(2)
        turn_x(3)
        perm_w1(1)
        perm_w1s(1)
        mm_l1(0, 0)
        relu(0, 0, "s")
        lace(0, 0, "s")
        mm_l1(0, 1)
        relu(0, 1, "s")
        for i in range(2, 4):
            scale_x(i, 0, "v")
            scale_x(i, 1, "v")
        quant_x(1)
        mm_l1(1, 0)
        relu(1, 0, "s")
        mm_l1(1, 1)
        relu(1, 1, "s")
        perm_w2s(0)
        perm_w2(0, 0)
        lace(0, 1, "v")
        quant_h(0, 0)
        quant_h(0, 1)
        ser_mm(0, 0)
        ser_tanh(0, 0)
        perm_w2(0, 1)
        ser_mm(0, 1)
        ser_tanh(0, 1)
        lace(1, 0, "v")
        lace(1, 1, "v")
        perm_w2(0, 2)
        ser_mm(0, 2)
        ser_tanh(0, 2)
        quant_h(1, 0)
        perm_w2(0, 3)
        ser_mm(0, 3)
        ser_tanh(0, 3)
        quant_h(1, 1)
        for b in range(4):
            ser_mm(1, b)
            ser_tanh(1, b)

        square(0, 0, 2, "v")
        square(0, 2, 4, "v")
        perm_w2s(1)
        perm_w2(1, 0)
        perm_w2(1, 1)
        square(1, 0, 2, "v")
        perm_w2(1, 2)
        square(1, 2, 4, "v")
        perm_w2(1, 3)
        for uh in range(2):
            for k in range(4):
                step_mm(DOP, uh, k)
                step_tanh(DOP, uh, k)
        for b in range(4):
            rsqrt(b)
        for uh in range(2):
            for i in range(4):
                step_tr(SER, uh, i, "v")
        for k in range(4):
            step_mm(GLU, 0, k)
        steps = [(DOP, 0), (DOP, 1), (GLU, 0), (GLU, 1), (GAB, 0), (GAB, 1)]
        for n in range(len(steps) + 1):
            if n < len(steps):
                for k in range(4):
                    step_mul(*steps[n], k, k + 1, "v")
            if n >= 1:
                for i in range(4):
                    step_tr(*steps[n - 1], i, "vsvs"[i])
                if n + 2 < len(steps):
                    for k in range(4):
                        step_mm(*steps[n + 2], k)
            if n + 2 < len(steps):
                for k in range(4):
                    step_tanh(*steps[n + 2], k)
